import numpy as np
import ml_dtypes


def mxq(x, axis, fmt="e4m3"):
    dtype, down = {"e4m3": (ml_dtypes.float8_e4m3fn, 7), "e5m2": (ml_dtypes.float8_e5m2, 14)}[fmt]
    v = np.moveaxis(np.asarray(x, np.float32).astype(ml_dtypes.bfloat16).astype(np.float64), axis, -1)
    blocks = v.reshape(v.shape[:-1] + (-1, 32))
    amax = np.abs(blocks).max(-1, keepdims=True)
    byte = np.maximum(np.where(amax > 0, np.frexp(amax)[1] - 1 + 127, 0) - down, 1)
    scale = np.exp2(byte - 127.0)
    codes = (blocks / scale).astype(np.float32).astype(dtype).astype(np.float64)
    return np.moveaxis((codes * scale).reshape(v.shape), -1, axis)


WIDE = False


def mx_kscale(k):
    if not WIDE:
        return np.ones(k)
    levels = np.array([10, -10, 5, -5, 0])
    a = np.random.permutation(np.resize(levels, k // 512 * 4)).reshape(k // 512, 4)
    idx = np.arange(k)
    return np.exp2(a[idx // 512, idx % 128 // 32])


BF16 = ml_dtypes.bfloat16


def bf(x):
    return np.asarray(x, np.float32).astype(BF16)


def f64(x):
    return np.asarray(x).astype(np.float64)


B, T, E, H = 4, 1024, 512, 1
SW = np.sqrt(2.0) * (T / E) ** 0.25 / np.sqrt(E)


def setup_inputs():
    s = mx_kscale(E)
    return {"x": bf(np.random.standard_normal((B, T, E)) * s),
            "wq": bf(np.random.standard_normal((H, E, E)) * SW / s[:, None]),
            "wk": bf(np.random.standard_normal((H, E, E)) * SW / s[:, None])}


def reference(x, wq, wk):
    xq = mxq(f64(x)[None], 3, "e4m3")
    q = xq @ mxq(f64(wq)[:, None], 2, "e4m3")
    k = xq @ mxq(f64(wk)[:, None], 2, "e4m3")
    k_rs = k.reshape(H, B, E, T)
    return (mxq(q, 3, "e4m3") @ mxq(k_rs, 2, "e4m3")) / np.sqrt(T)

@@ -1,0 +1,175 @@
+from contextlib import ExitStack
+
+import concourse.mybir as mybir
+from concourse.masks import make_identity
+
+F32 = mybir.dt.float32
+BF16 = mybir.dt.bfloat16
+U32 = mybir.dt.uint32
+U8 = mybir.dt.uint8
+FP8X4 = mybir.dt.float8_e4m3fn_x4
+COPY = mybir.ActivationFunctionType.Copy
+
+B, T, E = 4, 1024, 512
+P = 128
+FLOPS = 2 * B * T * E * E * 2 + 2 * B * T * E * T
+STEPS = 4
+KEY_BANKS = {1: (0, 1, 2), 2: (3, 4, 5), 3: (6, 7)}
+
+
+def tile_multiheadattention_pa_t_kernel(tc, x, wq, wk, out):
+    nc = tc.nc
+    with ExitStack() as ctx:
+        const = ctx.enter_context(tc.tile_pool(name="const", bufs=1))
+        work = ctx.enter_context(tc.tile_pool(name="work", bufs=2))
+        outp = ctx.enter_context(tc.tile_pool(name="outp", bufs=6))
+        psum = ctx.enter_context(tc.psum_pool(name="psum", bufs=8))
+        ctx.enter_context(tc.manual_schedule())
+
+        def empty(on_vector, dst, src, scale=None):
+            if on_vector and scale is None:
+                nc.vector.tensor_copy(out=dst, in_=src)
+            elif on_vector:
+                nc.vector.tensor_scalar_mul(out=dst, in0=src, scalar1=scale)
+            elif scale is None:
+                nc.scalar.copy(out=dst, in_=src)
+            else:
+                nc.scalar.activation(out=dst, in_=src, func=COPY, scale=scale)
+
+        def quantise(codes, scales, src):
+            nc.vector.quantize_mx(out=codes.bitcast(FP8X4), scales=scales, in_=src)
+
+        def mx(dst, lc, lsc, rc, rsc):
+            nc.tensor.matmul_mx(out=dst, lhsT=lc.bitcast(FP8X4), lhsT_scale=lsc,
+                                rhs=rc.bitcast(FP8X4), rhs_scale=rsc, start=True, stop=True)
+
+        x_sb = [const.tile([P, 4096], BF16, name="x_sb%d" % b) for b in range(B)]
+        w_sb = {w: const.tile([P, 2048], BF16, name="w_sb_%s" % w) for w in ("k", "q")}
+        xv = [x[b].rearrange("(p r) k -> p (r k)", r=8) for b in range(B)]
+        ov = [out[0, b].rearrange("(p r) j -> p (r j)", r=8) for b in range(B)]
+        nc.sync.dma_start(out=x_sb[0][:, 0:2048], in_=xv[0][:, 0:2048])
+        nc.sync.dma_start(out=x_sb[0][:, 2048:4096], in_=xv[0][:, 2048:4096])
+        for w, wd in (("k", wk), ("q", wq)):
+            nc.sync.dma_start(
+                out=w_sb[w][:].rearrange("p (u f) -> p u f", u=2),
+                in_=wd[0].rearrange("(u p e) c -> p u (e c)", u=2, e=2),
+            )
+        for b in range(1, B):
+            nc.sync.dma_start(out=x_sb[b][:], in_=xv[b])
+
+        warm = const.tile([P, 8], F32, name="warm")
+        nc.vector.memset(warm[:], 0.0)
+        nc.scalar.activation(out=warm[:], in_=warm[:], func=COPY, scale=1.0)
+        ident = const.tile([P, P], F32, name="ident")
+        make_identity(nc, ident[:])
+
+        gw = {w: const.tile([P, 2048], BF16, name="gw_%s" % w, align_bytes=64) for w in ("k", "q")}
+        wc = {w: const.tile([P, 512], U32, name="wc_%s" % w, align_bytes=64) for w in ("k", "q")}
+        ws = {w: const.tile([P, 512], U8, name="ws_%s" % w, align_bytes=64) for w in ("k", "q")}
+
+        grouped, codes, scales = {}, {}, {}
+
+        def alloc(kind, b):
+            grouped[kind, b] = work.tile([P, 4096], BF16, name="g%s%d" % (kind, b), tag="g" + kind, align_bytes=64)
+            codes[kind, b] = work.tile([P, 1024], U32, name="c%s%d" % (kind, b), tag="c" + kind, align_bytes=64)
+            scales[kind, b] = work.tile([P, 1024], U8, name="s%s%d" % (kind, b), tag="s" + kind, align_bytes=64)
+
+        def quantise_cols(kind, b, lo, hi):
+            quantise(codes[kind, b][:, lo:hi], scales[kind, b][:, lo:hi], grouped[kind, b][:, 4 * lo:4 * hi])
+
+        def operand(kind, b, lo, hi):
+            return codes[kind, b][:, lo:hi], scales[kind, b][:, lo:hi]
+
+        def transposes(b, a, on_vector):
+            if a == 0:
+                alloc("x", b)
+            bank = psum.tile([P, 512], F32, name="bank", tag="bank")
+            xw = x_sb[b][:].bitcast(F32)
+            for u in range(2):
+                for rr in range(2):
+                    o0 = u * 256 + rr * 128
+                    i0 = (2 * a + rr) * 256 + u * 128
+                    nc.tensor.transpose(bank[:, o0:o0 + 128], xw[:, i0:i0 + 128], ident[:])
+            dst = grouped["x", b][:].bitcast(F32)[:, a * 512:(a + 1) * 512]
+            empty(on_vector, dst.rearrange("p (t u) -> p t u", u=2), bank[:].rearrange("p (u t) -> p t u", u=2))
+
+        def keys(b, i, on_vector):
+            if i == 0:
+                alloc("k", b)
+            h, es = divmod(i, 4)
+            bank = psum.tile([P, 512], F32, name="bank", tag="bank")
+            for u in range(4):
+                r = 2 * u + h
+                xc, xs = operand("x", b, r * 128, (r + 1) * 128)
+                mx(bank[:, u * 128:(u + 1) * 128], xc, xs,
+                   wc["k"][:, es * 128:(es + 1) * 128], ws["k"][:, es * 128:(es + 1) * 128])
+            empty(on_vector, grouped["k", b][:, i * 512:(i + 1) * 512].rearrange("p (n u) -> p n u", u=4),
+                  bank[:].rearrange("p (u n) -> p n u", u=4))
+
+        def queries(b, r, on_vector):
+            if r == 0:
+                alloc("q", b)
+            bank = psum.tile([P, 512], F32, name="bank", tag="bank")
+            xc, xs = operand("x", b, r * 128, (r + 1) * 128)
+            for u in range(4):
+                mx(bank[:, u * 128:(u + 1) * 128],
+                   wc["q"][:, u * 128:(u + 1) * 128], ws["q"][:, u * 128:(u + 1) * 128], xc, xs)
+            empty(on_vector, grouped["q", b][:, r * 512:(r + 1) * 512].rearrange("p (n u) -> p n u", u=4),
+                  bank[:].rearrange("p (u n) -> p n u", u=4))
+
+        def scores(b, r, h, o, on_vector):
+            bank = psum.tile([P, 512], F32, name="bank", tag="bank")
+            qc, qs = operand("q", b, r * 128, (r + 1) * 128)
+            kc, ks = operand("k", b, h * 512, (h + 1) * 512)
+            mx(bank[:], qc, qs, kc, ks)
+            c0 = (r % 2) * 1024 + h * 512
+            empty(on_vector, o[:, c0:c0 + 512], bank[:], scale=1.0 / 32.0)
+
+        def weights():
+            src_w = "p (t c i) -> p c t i"
+            nc.vector.tensor_copy(out=gw["k"][:].rearrange("p (c i t) -> p c t i", i=4, t=4),
+                                  in_=w_sb["k"][:].rearrange(src_w, t=4, i=4))
+            nc.scalar.copy(out=gw["q"][:].rearrange("p (i c t) -> p c t i", i=4, t=4),
+                           in_=w_sb["q"][:].rearrange(src_w, t=4, i=4))
+
+        for g in range(-STEPS, B * STEPS):
+            b, s = divmod(g, STEPS)
+            head = b < 0
+            ahead = b + 1 < B
+            nxt = 0 <= g + 1 < B * STEPS
+            qb, qp = divmod(g + 1, STEPS)
+            if nxt:
+                queries(qb, 2 * qp, not head)
+                queries(qb, 2 * qp + 1, not head)
+            if ahead and s == 0:
+                for a in range(4):
+                    transposes(b + 1, a, a == 0 if head else a % 2 == 0)
+            if g == -STEPS:
+                quantise_cols("x", 0, 0, 512)
+                weights()
+                quantise(wc["k"][:], ws["k"][:], gw["k"][:])
+                quantise_cols("x", 0, 512, 1024)
+            if not head:
+                o = outp.tile([P, 2048], F32, name="o", tag="o")
+                scores(b, 2 * s, 0, o, False)
+                scores(b, 2 * s, 1, o, not (ahead or nxt))
+                if not ahead:
+                    nc.sync.dma_start(out=ov[b][:, s * 2048:s * 2048 + 1024], in_=o[:, 0:1024])
+            if nxt:
+                quantise_cols("q", qb, qp * 256, (qp + 1) * 256)
+            if ahead and s == 0 and not head:
+                quantise_cols("x", b + 1, 0, 1024)
+            if not head:
+                scores(b, 2 * s + 1, 0, o, False)
+                scores(b, 2 * s + 1, 1, o, not ahead)
+                if ahead:
+                    nc.sync.dma_start(out=ov[b][:, s * 2048:(s + 1) * 2048], in_=o[:])
+                else:
+                    nc.sync.dma_start(out=ov[b][:, s * 2048 + 1024:(s + 1) * 2048], in_=o[:, 1024:2048])
+            if ahead and s > 0:
+                for j, i in enumerate(KEY_BANKS[s]):
+                    keys(b + 1, i, i % 2 == 1 if head else j > 0)
+                if g == 1 - STEPS:
+                    quantise(wc["q"][:], ws["q"][:], gw["q"][:])
+                if s >= 2:
+                    quantise_cols("k", b + 1, (s - 2) * 512, (s - 1) * 512)

@@ -13,8 +13,10 @@ COPY = mybir.ActivationFunctionType.Copy
 B, T, E = 4, 1024, 512
 P = 128
 FLOPS = 2 * B * T * E * E * 2 + 2 * B * T * E * T
-STEPS = 4
-KEY_BANKS = {1: (0, 1, 2), 2: (3, 4, 5), 3: (6, 7)}
+STEPS = 4 * B
+Q_AHEAD = 1
+K_AHEAD = 4
+X_AHEAD = 6
 
 
 def tile_multiheadattention_pa_t_kernel(tc, x, wq, wk, out):
@@ -22,7 +24,7 @@ def tile_multiheadattention_pa_t_kernel(tc, x, wq, wk, out):
     with ExitStack() as ctx:
         const = ctx.enter_context(tc.tile_pool(name="const", bufs=1))
         work = ctx.enter_context(tc.tile_pool(name="work", bufs=2))
-        outp = ctx.enter_context(tc.tile_pool(name="outp", bufs=6))
+        outp = ctx.enter_context(tc.tile_pool(name="outp", bufs=12))
         psum = ctx.enter_context(tc.psum_pool(name="psum", bufs=8))
         ctx.enter_context(tc.manual_schedule())
 
@@ -36,8 +38,8 @@ def tile_multiheadattention_pa_t_kernel(tc, x, wq, wk, out):
             else:
                 nc.scalar.activation(out=dst, in_=src, func=COPY, scale=scale)
 
-        def quantise(codes, scales, src):
-            nc.vector.quantize_mx(out=codes.bitcast(FP8X4), scales=scales, in_=src)
+        def quantise(words, plane, src):
+            nc.vector.quantize_mx(out=words.bitcast(FP8X4), scales=plane, in_=src)
 
         def mx(dst, lc, lsc, rc, rsc):
             nc.tensor.matmul_mx(out=dst, lhsT=lc.bitcast(FP8X4), lhsT_scale=lsc,
@@ -122,54 +124,50 @@ def tile_multiheadattention_pa_t_kernel(tc, x, wq, wk, out):
             qc, qs = operand("q", b, r * 128, (r + 1) * 128)
             kc, ks = operand("k", b, h * 512, (h + 1) * 512)
             mx(bank[:], qc, qs, kc, ks)
-            c0 = (r % 2) * 1024 + h * 512
-            empty(on_vector, o[:, c0:c0 + 512], bank[:], scale=1.0 / 32.0)
+            empty(on_vector, o[:, h * 512:(h + 1) * 512], bank[:], scale=1.0 / 32.0)
 
-        def weights():
+        def regroup_weights():
             src_w = "p (t c i) -> p c t i"
             nc.vector.tensor_copy(out=gw["k"][:].rearrange("p (c i t) -> p c t i", i=4, t=4),
                                   in_=w_sb["k"][:].rearrange(src_w, t=4, i=4))
             nc.scalar.copy(out=gw["q"][:].rearrange("p (i c t) -> p c t i", i=4, t=4),
                            in_=w_sb["q"][:].rearrange(src_w, t=4, i=4))
 
-        for g in range(-STEPS, B * STEPS):
-            b, s = divmod(g, STEPS)
-            head = b < 0
-            ahead = b + 1 < B
-            nxt = 0 <= g + 1 < B * STEPS
-            qb, qp = divmod(g + 1, STEPS)
-            if nxt:
+        for g in range(-X_AHEAD, STEPS):
+            head = g < 0
+            do_q = 0 <= g + Q_AHEAD < STEPS
+            do_k = 0 <= g + K_AHEAD < STEPS
+            do_x = (g + X_AHEAD) % 4 == 0 and (g + X_AHEAD) // 4 < B
+            qb, qp = divmod(g + Q_AHEAD, 4)
+            kb, kp = divmod(g + K_AHEAD, 4)
+            xb = (g + X_AHEAD) // 4
+            if do_q:
                 queries(qb, 2 * qp, not head)
                 queries(qb, 2 * qp + 1, not head)
-            if ahead and s == 0:
+            if do_k:
+                keys(kb, 2 * kp, do_x and not head)
+                keys(kb, 2 * kp + 1, True)
+            if do_x:
                 for a in range(4):
-                    transposes(b + 1, a, a == 0 if head else a % 2 == 0)
-            if g == -STEPS:
-                quantise_cols("x", 0, 0, 512)
-                weights()
-                quantise(wc["k"][:], ws["k"][:], gw["k"][:])
-                quantise_cols("x", 0, 512, 1024)
-            if not head:
-                o = outp.tile([P, 2048], F32, name="o", tag="o")
-                scores(b, 2 * s, 0, o, False)
-                scores(b, 2 * s, 1, o, not (ahead or nxt))
-                if not ahead:
-                    nc.sync.dma_start(out=ov[b][:, s * 2048:s * 2048 + 1024], in_=o[:, 0:1024])
-            if nxt:
+                    transposes(xb, a, a == 0 if xb == 0 else a % 2 == 0)
+            if do_q:
                 quantise_cols("q", qb, qp * 256, (qp + 1) * 256)
-            if ahead and s == 0 and not head:
-                quantise_cols("x", b + 1, 0, 1024)
+            if do_k:
+                quantise_cols("k", kb, kp * 256, (kp + 1) * 256)
+            if do_x and xb == 0:
+                quantise_cols("x", 0, 0, 512)
+                regroup_weights()
+                quantise_cols("x", 0, 512, 1024)
+                quantise(wc["k"][:], ws["k"][:], gw["k"][:])
+            elif do_x:
+                quantise_cols("x", xb, 0, 1024)
+            if g == 1 - X_AHEAD:
+                quantise(wc["q"][:], ws["q"][:], gw["q"][:])
             if not head:
-                scores(b, 2 * s + 1, 0, o, False)
-                scores(b, 2 * s + 1, 1, o, not ahead)
-                if ahead:
-                    nc.sync.dma_start(out=ov[b][:, s * 2048:(s + 1) * 2048], in_=o[:])
-                else:
-                    nc.sync.dma_start(out=ov[b][:, s * 2048 + 1024:(s + 1) * 2048], in_=o[:, 1024:2048])
-            if ahead and s > 0:
-                for j, i in enumerate(KEY_BANKS[s]):
-                    keys(b + 1, i, i % 2 == 1 if head else j > 0)
-                if g == 1 - STEPS:
-                    quantise(wc["q"][:], ws["q"][:], gw["q"][:])
-                if s >= 2:
-                    quantise_cols("k", b + 1, (s - 2) * 512, (s - 1) * 512)
+                b, s = divmod(g, 4)
+                for rr in range(2):
+                    r = 2 * s + rr
+                    o = outp.tile([P, 1024], F32, name="o", tag="o")
+                    scores(b, r, 0, o, False)
+                    scores(b, r, 1, o, not do_k and (rr == 1 or not do_q))
+                    nc.sync.dma_start(out=ov[b][:, r * 1024:(r + 1) * 1024], in_=o[:])

@@ -145,11 +145,11 @@ def tile_multiheadattention_pa_t_kernel(tc, x, wq, wk, out):
                 queries(qb, 2 * qp, not head)
                 queries(qb, 2 * qp + 1, not head)
             if do_k:
-                keys(kb, 2 * kp, do_x and not head)
+                keys(kb, 2 * kp, g > 4 * (B - 1) - X_AHEAD and g % 2 == 0)
                 keys(kb, 2 * kp + 1, True)
             if do_x:
                 for a in range(4):
-                    transposes(xb, a, a == 0 if xb == 0 else a % 2 == 0)
+                    transposes(xb, a, a == 0 if xb == 0 else a % 2 == 1)
             if do_q:
                 quantise_cols("q", qb, qp * 256, (qp + 1) * 256)
             if do_k:

@@ -49,13 +49,21 @@ def tile_multiheadattention_pa_t_kernel(tc, x, wq, wk, out):
         w_sb = {w: const.tile([P, 2048], BF16, name="w_sb_%s" % w) for w in ("k", "q")}
         xv = [x[b].rearrange("(p r) k -> p (r k)", r=8) for b in range(B)]
         ov = [out[0, b].rearrange("(p r) j -> p (r j)", r=8) for b in range(B)]
-        nc.sync.dma_start(out=x_sb[0][:, 0:2048], in_=xv[0][:, 0:2048])
-        nc.sync.dma_start(out=x_sb[0][:, 2048:4096], in_=xv[0][:, 2048:4096])
-        for w, wd in (("k", wk), ("q", wq)):
+
+        def load_x0(a):
+            nc.sync.dma_start(out=x_sb[0][:, a * 1024:(a + 1) * 1024], in_=xv[0][:, a * 1024:(a + 1) * 1024])
+
+        def load_w(w, wd):
             nc.sync.dma_start(
                 out=w_sb[w][:].rearrange("p (u f) -> p u f", u=2),
                 in_=wd[0].rearrange("(u p e) c -> p u (e c)", u=2, e=2),
             )
+        load_x0(0)
+        load_x0(1)
+        load_w("k", wk)
+        load_x0(2)
+        load_x0(3)
+        load_w("q", wq)
         for b in range(1, B):
             nc.sync.dma_start(out=x_sb[b][:], in_=xv[b])
 
@@ -126,12 +134,10 @@ def tile_multiheadattention_pa_t_kernel(tc, x, wq, wk, out):
             mx(bank[:], qc, qs, kc, ks)
             empty(on_vector, o[:, h * 512:(h + 1) * 512], bank[:], scale=1.0 / 32.0)
 
-        def regroup_weights():
-            src_w = "p (t c i) -> p c t i"
-            nc.vector.tensor_copy(out=gw["k"][:].rearrange("p (c i t) -> p c t i", i=4, t=4),
-                                  in_=w_sb["k"][:].rearrange(src_w, t=4, i=4))
-            nc.scalar.copy(out=gw["q"][:].rearrange("p (i c t) -> p c t i", i=4, t=4),
-                           in_=w_sb["q"][:].rearrange(src_w, t=4, i=4))
+        def regroup(copy, w, lo, hi):
+            dst = gw[w][:].rearrange("p (c i t) -> p c t i" if w == "k" else "p (i c t) -> p c t i", i=4, t=4)
+            src = w_sb[w][:].rearrange("p (t c i) -> p c t i", t=4, i=4)
+            copy(out=dst[:, lo:hi], in_=src[:, lo:hi])
 
         for g in range(-X_AHEAD, STEPS):
             head = g < 0
@@ -146,23 +152,29 @@ def tile_multiheadattention_pa_t_kernel(tc, x, wq, wk, out):
                 queries(qb, 2 * qp + 1, not head)
             if do_k:
                 keys(kb, 2 * kp, g > 4 * (B - 1) - X_AHEAD and g % 2 == 0)
-                keys(kb, 2 * kp + 1, True)
-            if do_x:
+                keys(kb, 2 * kp + 1, not head or g % 2 == 0)
+            if do_x and xb == 0:
+                transposes(0, 0, False)
+                transposes(0, 1, True)
+                regroup(nc.vector.tensor_copy, "k", 0, 96)
+                regroup(nc.scalar.copy, "k", 96, 128)
+                quantise_cols("x", 0, 0, 512)
+                transposes(0, 2, False)
+                transposes(0, 3, False)
+                quantise(wc["k"][:], ws["k"][:], gw["k"][:])
+                regroup(nc.scalar.copy, "q", 0, 32)
+                quantise_cols("x", 0, 512, 1024)
+                regroup(nc.vector.tensor_copy, "q", 32, 128)
+                quantise(wc["q"][:], ws["q"][:], gw["q"][:])
+            elif do_x:
                 for a in range(4):
-                    transposes(xb, a, a == 0 if xb == 0 else a % 2 == 1)
+                    transposes(xb, a, a % 2 == 1)
             if do_q:
                 quantise_cols("q", qb, qp * 256, (qp + 1) * 256)
             if do_k:
                 quantise_cols("k", kb, kp * 256, (kp + 1) * 256)
-            if do_x and xb == 0:
-                quantise_cols("x", 0, 0, 512)
-                regroup_weights()
-                quantise_cols("x", 0, 512, 1024)
-                quantise(wc["k"][:], ws["k"][:], gw["k"][:])
-            elif do_x:
+            if do_x and xb > 0:
                 quantise_cols("x", xb, 0, 1024)
-            if g == 1 - X_AHEAD:
-                quantise(wc["q"][:], ws["q"][:], gw["q"][:])
             if not head:
                 b, s = divmod(g, 4)
                 for rr in range(2):

@@ -67,6 +67,8 @@ def tile_multiheadattention_pa_t_kernel(tc, x, wq, wk, out):
         for b in range(1, B):
             nc.sync.dma_start(out=x_sb[b][:], in_=xv[b])
 
+        zeros = const.tile([P, 512], BF16, name="zeros")
+        nc.vector.memset(zeros[:], 0.0)
         warm = const.tile([P, 8], F32, name="warm")
         nc.vector.memset(warm[:], 0.0)
         nc.scalar.activation(out=warm[:], in_=warm[:], func=COPY, scale=1.0)
@@ -89,6 +91,11 @@ def tile_multiheadattention_pa_t_kernel(tc, x, wq, wk, out):
 
         def operand(kind, b, lo, hi):
             return codes[kind, b][:, lo:hi], scales[kind, b][:, lo:hi]
+
+        def spin(n):
+            bank = psum.tile([P, 512], F32, name="bank", tag="bank")
+            for i in range(n):
+                nc.tensor.matmul(out=bank[:], lhsT=zeros[:, 0:P], rhs=zeros[:], start=True, stop=True)
 
         def transposes(b, a, on_vector):
             if a == 0:
@@ -154,13 +161,16 @@ def tile_multiheadattention_pa_t_kernel(tc, x, wq, wk, out):
                 keys(kb, 2 * kp, g > 4 * (B - 1) - X_AHEAD and g % 2 == 0)
                 keys(kb, 2 * kp + 1, not head or g % 2 == 0)
             if do_x and xb == 0:
+                spin(5)
                 transposes(0, 0, False)
                 transposes(0, 1, True)
+                spin(2)
                 regroup(nc.vector.tensor_copy, "k", 0, 96)
                 regroup(nc.scalar.copy, "k", 96, 128)
                 quantise_cols("x", 0, 0, 512)
                 transposes(0, 2, False)
                 transposes(0, 3, False)
+                spin(3)
                 quantise(wc["k"][:], ws["k"][:], gw["k"][:])
                 regroup(nc.scalar.copy, "q", 0, 32)
                 quantise_cols("x", 0, 512, 1024)

@@ -68,7 +68,7 @@ def tile_multiheadattention_pa_t_kernel(tc, x, wq, wk, out):
             nc.sync.dma_start(out=x_sb[b][:], in_=xv[b])
 
         zeros = const.tile([P, 512], BF16, name="zeros")
-        nc.vector.memset(zeros[:], 0.0)
+        nc.vector.memset(zeros[:].bitcast(mybir.dt.int32), 0)
         warm = const.tile([P, 8], F32, name="warm")
         nc.vector.memset(warm[:], 0.0)
         nc.scalar.activation(out=warm[:], in_=warm[:], func=COPY, scale=1.0)
@@ -178,7 +178,7 @@ def tile_multiheadattention_pa_t_kernel(tc, x, wq, wk, out):
                 quantise(wc["q"][:], ws["q"][:], gw["q"][:])
             elif do_x:
                 for a in range(4):
-                    transposes(xb, a, a % 2 == 1)
+                    transposes(xb, a, a != 0 if xb > 1 else a % 2 == 1)
             if do_q:
                 quantise_cols("q", qb, qp * 256, (qp + 1) * 256)
             if do_k:

@@ -24,7 +24,7 @@ def tile_multiheadattention_pa_t_kernel(tc, x, wq, wk, out):
     with ExitStack() as ctx:
         const = ctx.enter_context(tc.tile_pool(name="const", bufs=1))
         work = ctx.enter_context(tc.tile_pool(name="work", bufs=2))
-        outp = ctx.enter_context(tc.tile_pool(name="outp", bufs=12))
+        outp = ctx.enter_context(tc.tile_pool(name="outp", bufs=6))
         psum = ctx.enter_context(tc.psum_pool(name="psum", bufs=8))
         ctx.enter_context(tc.manual_schedule())
 
@@ -178,7 +178,7 @@ def tile_multiheadattention_pa_t_kernel(tc, x, wq, wk, out):
                 quantise(wc["q"][:], ws["q"][:], gw["q"][:])
             elif do_x:
                 for a in range(4):
-                    transposes(xb, a, a != 0 if xb > 1 else a % 2 == 1)
+                    transposes(xb, a, a % 2 == 1)
             if do_q:
                 quantise_cols("q", qb, qp * 256, (qp + 1) * 256)
             if do_k:
@@ -187,9 +187,17 @@ def tile_multiheadattention_pa_t_kernel(tc, x, wq, wk, out):
                 quantise_cols("x", xb, 0, 1024)
             if not head:
                 b, s = divmod(g, 4)
+                oo = outp.tile([P, 2048], F32, name="o", tag="o")
                 for rr in range(2):
                     r = 2 * s + rr
-                    o = outp.tile([P, 1024], F32, name="o", tag="o")
+                    o = oo[:, rr * 1024:(rr + 1) * 1024]
                     scores(b, r, 0, o, False)
+                    if g >= 99:
+                        nc.sync.dma_start(out=ov[b][:, r * 1024:r * 1024 + 512], in_=o[:, 0:512])
                     scores(b, r, 1, o, not do_k and (rr == 1 or not do_q))
-                    nc.sync.dma_start(out=ov[b][:, r * 1024:(r + 1) * 1024], in_=o[:])
+                    if g >= 99:
+                        nc.sync.dma_start(out=ov[b][:, r * 1024 + 512:(r + 1) * 1024], in_=o[:, 512:1024])
+                    elif g >= 99:
+                        nc.sync.dma_start(out=ov[b][:, r * 1024:(r + 1) * 1024], in_=o[:])
+                if g < 99:
+                    nc.sync.dma_start(out=ov[b][:, s * 2048:(s + 1) * 2048], in_=oo[:])

@@ -172,9 +172,9 @@ def tile_multiheadattention_pa_t_kernel(tc, x, wq, wk, out):
                 transposes(0, 3, False)
                 spin(3)
                 quantise(wc["k"][:], ws["k"][:], gw["k"][:])
-                regroup(nc.scalar.copy, "q", 0, 32)
+                regroup(nc.scalar.copy, "q", 0, 64)
                 quantise_cols("x", 0, 512, 1024)
-                regroup(nc.vector.tensor_copy, "q", 32, 128)
+                regroup(nc.vector.tensor_copy, "q", 64, 128)
                 quantise(wc["q"][:], ws["q"][:], gw["q"][:])
             elif do_x:
                 for a in range(4):
@@ -192,12 +192,8 @@ def tile_multiheadattention_pa_t_kernel(tc, x, wq, wk, out):
                     r = 2 * s + rr
                     o = oo[:, rr * 1024:(rr + 1) * 1024]
                     scores(b, r, 0, o, False)
-                    if g >= 99:
-                        nc.sync.dma_start(out=ov[b][:, r * 1024:r * 1024 + 512], in_=o[:, 0:512])
                     scores(b, r, 1, o, not do_k and (rr == 1 or not do_q))
-                    if g >= 99:
-                        nc.sync.dma_start(out=ov[b][:, r * 1024 + 512:(r + 1) * 1024], in_=o[:, 512:1024])
-                    elif g >= 99:
+                    if not (not do_k):
                         nc.sync.dma_start(out=ov[b][:, r * 1024:(r + 1) * 1024], in_=o[:])
-                if g < 99:
+                if not do_k:
                     nc.sync.dma_start(out=ov[b][:, s * 2048:(s + 1) * 2048], in_=oo[:])

from contextlib import ExitStack

import concourse.mybir as mybir
from concourse.masks import make_identity

F32 = mybir.dt.float32
BF16 = mybir.dt.bfloat16
U32 = mybir.dt.uint32
U8 = mybir.dt.uint8
FP8X4 = mybir.dt.float8_e4m3fn_x4
COPY = mybir.ActivationFunctionType.Copy

B, T, E = 4, 1024, 512
P = 128
FLOPS = 2 * B * T * E * E * 2 + 2 * B * T * E * T
STEPS = 4 * B
Q_AHEAD = 1
K_AHEAD = 4
X_AHEAD = 6


def tile_multiheadattention_pa_t_kernel(tc, x, wq, wk, out):
    nc = tc.nc
    with ExitStack() as ctx:
        const = ctx.enter_context(tc.tile_pool(name="const", bufs=1))
        work = ctx.enter_context(tc.tile_pool(name="work", bufs=2))
        outp = ctx.enter_context(tc.tile_pool(name="outp", bufs=6))
        psum = ctx.enter_context(tc.psum_pool(name="psum", bufs=8))
        ctx.enter_context(tc.manual_schedule())

        def empty(on_vector, dst, src, scale=None):
            if on_vector and scale is None:
                nc.vector.tensor_copy(out=dst, in_=src)
            elif on_vector:
                nc.vector.tensor_scalar_mul(out=dst, in0=src, scalar1=scale)
            elif scale is None:
                nc.scalar.copy(out=dst, in_=src)
            else:
                nc.scalar.activation(out=dst, in_=src, func=COPY, scale=scale)

        def quantise(words, plane, src):
            nc.vector.quantize_mx(out=words.bitcast(FP8X4), scales=plane, in_=src)

        def mx(dst, lc, lsc, rc, rsc):
            nc.tensor.matmul_mx(out=dst, lhsT=lc.bitcast(FP8X4), lhsT_scale=lsc,
                                rhs=rc.bitcast(FP8X4), rhs_scale=rsc, start=True, stop=True)

        x_sb = [const.tile([P, 4096], BF16, name="x_sb%d" % b) for b in range(B)]
        w_sb = {w: const.tile([P, 2048], BF16, name="w_sb_%s" % w) for w in ("k", "q")}
        xv = [x[b].rearrange("(p r) k -> p (r k)", r=8) for b in range(B)]
        ov = [out[0, b].rearrange("(p r) j -> p (r j)", r=8) for b in range(B)]

        def load_x0(a):
            nc.sync.dma_start(out=x_sb[0][:, a * 1024:(a + 1) * 1024], in_=xv[0][:, a * 1024:(a + 1) * 1024])

        def load_w(w, wd):
            nc.sync.dma_start(
                out=w_sb[w][:].rearrange("p (u f) -> p u f", u=2),
                in_=wd[0].rearrange("(u p e) c -> p u (e c)", u=2, e=2),
            )
        load_x0(0)
        load_x0(1)
        load_w("k", wk)
        load_x0(2)
        load_x0(3)
        load_w("q", wq)
        for b in range(1, B):
            nc.sync.dma_start(out=x_sb[b][:], in_=xv[b])

        zeros = const.tile([P, 512], BF16, name="zeros")
        nc.vector.memset(zeros[:].bitcast(mybir.dt.int32), 0)
        warm = const.tile([P, 8], F32, name="warm")
        nc.vector.memset(warm[:], 0.0)
        nc.scalar.activation(out=warm[:], in_=warm[:], func=COPY, scale=1.0)
        ident = const.tile([P, P], F32, name="ident")
        make_identity(nc, ident[:])

        gw = {w: const.tile([P, 2048], BF16, name="gw_%s" % w, align_bytes=64) for w in ("k", "q")}
        wc = {w: const.tile([P, 512], U32, name="wc_%s" % w, align_bytes=64) for w in ("k", "q")}
        ws = {w: const.tile([P, 512], U8, name="ws_%s" % w, align_bytes=64) for w in ("k", "q")}

        grouped, codes, scales = {}, {}, {}

        def alloc(kind, b):
            grouped[kind, b] = work.tile([P, 4096], BF16, name="g%s%d" % (kind, b), tag="g" + kind, align_bytes=64)
            codes[kind, b] = work.tile([P, 1024], U32, name="c%s%d" % (kind, b), tag="c" + kind, align_bytes=64)
            scales[kind, b] = work.tile([P, 1024], U8, name="s%s%d" % (kind, b), tag="s" + kind, align_bytes=64)

        def quantise_cols(kind, b, lo, hi):
            quantise(codes[kind, b][:, lo:hi], scales[kind, b][:, lo:hi], grouped[kind, b][:, 4 * lo:4 * hi])

        def operand(kind, b, lo, hi):
            return codes[kind, b][:, lo:hi], scales[kind, b][:, lo:hi]

        def spin(n):
            bank = psum.tile([P, 512], F32, name="bank", tag="bank")
            for i in range(n):
                nc.tensor.matmul(out=bank[:], lhsT=zeros[:, 0:P], rhs=zeros[:], start=True, stop=True)

        def transposes(b, a, on_vector):
            if a == 0:
                alloc("x", b)
            bank = psum.tile([P, 512], F32, name="bank", tag="bank")
            xw = x_sb[b][:].bitcast(F32)
            for u in range(2):
                for rr in range(2):
                    o0 = u * 256 + rr * 128
                    i0 = (2 * a + rr) * 256 + u * 128
                    nc.tensor.transpose(bank[:, o0:o0 + 128], xw[:, i0:i0 + 128], ident[:])
            dst = grouped["x", b][:].bitcast(F32)[:, a * 512:(a + 1) * 512]
            empty(on_vector, dst.rearrange("p (t u) -> p t u", u=2), bank[:].rearrange("p (u t) -> p t u", u=2))

        def keys(b, i, on_vector):
            if i == 0:
                alloc("k", b)
            h, es = divmod(i, 4)
            bank = psum.tile([P, 512], F32, name="bank", tag="bank")
            for u in range(4):
                r = 2 * u + h
                xc, xs = operand("x", b, r * 128, (r + 1) * 128)
                mx(bank[:, u * 128:(u + 1) * 128], xc, xs,
                   wc["k"][:, es * 128:(es + 1) * 128], ws["k"][:, es * 128:(es + 1) * 128])
            empty(on_vector, grouped["k", b][:, i * 512:(i + 1) * 512].rearrange("p (n u) -> p n u", u=4),
                  bank[:].rearrange("p (u n) -> p n u", u=4))

        def queries(b, r, on_vector):
            if r == 0:
                alloc("q", b)
            bank = psum.tile([P, 512], F32, name="bank", tag="bank")
            xc, xs = operand("x", b, r * 128, (r + 1) * 128)
            for u in range(4):
                mx(bank[:, u * 128:(u + 1) * 128],
                   wc["q"][:, u * 128:(u + 1) * 128], ws["q"][:, u * 128:(u + 1) * 128], xc, xs)
            empty(on_vector, grouped["q", b][:, r * 512:(r + 1) * 512].rearrange("p (n u) -> p n u", u=4),
                  bank[:].rearrange("p (u n) -> p n u", u=4))

        def scores(b, r, h, o, on_vector):
            bank = psum.tile([P, 512], F32, name="bank", tag="bank")
            qc, qs = operand("q", b, r * 128, (r + 1) * 128)
            kc, ks = operand("k", b, h * 512, (h + 1) * 512)
            mx(bank[:], qc, qs, kc, ks)
            empty(on_vector, o[:, h * 512:(h + 1) * 512], bank[:], scale=1.0 / 32.0)

        def regroup(copy, w, lo, hi):
            dst = gw[w][:].rearrange("p (c i t) -> p c t i" if w == "k" else "p (i c t) -> p c t i", i=4, t=4)
            src = w_sb[w][:].rearrange("p (t c i) -> p c t i", t=4, i=4)
            copy(out=dst[:, lo:hi], in_=src[:, lo:hi])

        for g in range(-X_AHEAD, STEPS):
            head = g < 0
            do_q = 0 <= g + Q_AHEAD < STEPS
            do_k = 0 <= g + K_AHEAD < STEPS
            do_x = (g + X_AHEAD) % 4 == 0 and (g + X_AHEAD) // 4 < B
            qb, qp = divmod(g + Q_AHEAD, 4)
            kb, kp = divmod(g + K_AHEAD, 4)
            xb = (g + X_AHEAD) // 4
            if do_q:
                queries(qb, 2 * qp, not head)
                queries(qb, 2 * qp + 1, not head)
            if do_k:
                keys(kb, 2 * kp, g > 4 * (B - 1) - X_AHEAD and g % 2 == 0)
                keys(kb, 2 * kp + 1, not head or g % 2 == 0)
            if do_x and xb == 0:
                spin(5)
                transposes(0, 0, False)
                transposes(0, 1, True)
                spin(2)
                regroup(nc.vector.tensor_copy, "k", 0, 96)
                regroup(nc.scalar.copy, "k", 96, 128)
                quantise_cols("x", 0, 0, 512)
                transposes(0, 2, False)
                transposes(0, 3, False)
                spin(3)
                quantise(wc["k"][:], ws["k"][:], gw["k"][:])
                regroup(nc.scalar.copy, "q", 0, 64)
                quantise_cols("x", 0, 512, 1024)
                regroup(nc.vector.tensor_copy, "q", 64, 128)
                quantise(wc["q"][:], ws["q"][:], gw["q"][:])
            elif do_x:
                for a in range(4):
                    transposes(xb, a, a % 2 == 1)
            if do_q:
                quantise_cols("q", qb, qp * 256, (qp + 1) * 256)
            if do_k:
                quantise_cols("k", kb, kp * 256, (kp + 1) * 256)
            if do_x and xb > 0:
                quantise_cols("x", xb, 0, 1024)
            if not head:
                b, s = divmod(g, 4)
                oo = outp.tile([P, 2048], F32, name="o", tag="o")
                for rr in range(2):
                    r = 2 * s + rr
                    o = oo[:, rr * 1024:(rr + 1) * 1024]
                    scores(b, r, 0, o, False)
                    scores(b, r, 1, o, not do_k and (rr == 1 or not do_q))
                    if not (not do_k):
                        nc.sync.dma_start(out=ov[b][:, r * 1024:(r + 1) * 1024], in_=o[:])
                if not do_k:
                    nc.sync.dma_start(out=ov[b][:, s * 2048:(s + 1) * 2048], in_=oo[:])
